import numpy as np
import ml_dtypes


def mxq(x, axis, fmt="e4m3"):
    dtype, down = {"e4m3": (ml_dtypes.float8_e4m3fn, 7), "e5m2": (ml_dtypes.float8_e5m2, 14)}[fmt]
    v = np.moveaxis(np.asarray(x, np.float32).astype(ml_dtypes.bfloat16).astype(np.float64), axis, -1)
    blocks = v.reshape(v.shape[:-1] + (-1, 32))
    amax = np.abs(blocks).max(-1, keepdims=True)
    byte = np.maximum(np.where(amax > 0, np.frexp(amax)[1] - 1 + 127, 0) - down, 1)
    scale = np.exp2(byte - 127.0)
    codes = (blocks / scale).astype(np.float32).astype(dtype).astype(np.float64)
    return np.moveaxis((codes * scale).reshape(v.shape), -1, axis)


WIDE = False


def mx_kscale(k):
    if not WIDE:
        return np.ones(k)
    levels = np.array([20, -20, 10, -10, 0])
    a = np.random.permutation(np.resize(levels, k // 512 * 4)).reshape(k // 512, 4)
    idx = np.arange(k)
    return np.exp2(a[idx // 512, idx % 128 // 32])


BF16 = ml_dtypes.bfloat16


def bf(x):
    return np.asarray(x, np.float32).astype(BF16)


def f64(x):
    return np.asarray(x).astype(np.float64)


B, D, H = 2048, 1024, 256


def sigmoid(v):
    return 1.0 / (1.0 + np.exp(-v))


def xavier(rows, cols):
    limit = np.sqrt(6.0 / (rows + cols))
    return np.random.uniform(-limit, limit, (rows, cols))


def setup_inputs():
    u = mx_kscale(4 * H)[:H]
    x = bf(np.random.standard_normal((B, D)))
    h0 = bf(np.random.standard_normal((B, H)))
    c0 = bf(np.random.standard_normal((B, H)))
    inp = {"x": x, "h0": h0, "c0": c0}
    pre = []
    for n in ("i", "f", "g", "o"):
        wi = bf(xavier(H, D))
        bi = bf(np.random.standard_normal(H) * 0.1)
        wh = bf(xavier(H, H))
        bh = bf(np.random.standard_normal(H) * 0.1)
        pre.append(f64(x) @ f64(wi).T + f64(h0) @ f64(wh).T + f64(bi) + f64(bh))
        inp["W_i" + n] = bf(f64(wi) / u[:, None])
        inp["b_i" + n] = bi
        inp["W_h" + n] = wh
        inp["b_h" + n] = bh
    inp["gates"] = np.asarray(np.concatenate(pre, axis=1), np.float32)
    g = np.random.standard_normal((2, B, H)) * np.exp2(np.random.randint(-12, 1, (1, B, 1))) * 8.0 * u
    inp["grad_out"] = bf(g)
    return inp


def reference(x, h0, c0,
              W_ii, b_ii, W_hi, b_hi,
              W_if, b_if, W_hf, b_hf,
              W_ig, b_ig, W_hg, b_hg,
              W_io, b_io, W_ho, b_ho, gates, grad_out):
    a = f64(gates)
    c0f = f64(c0)
    i_t = sigmoid(a[:, 0 * H:1 * H])
    f_t = sigmoid(a[:, 1 * H:2 * H])
    g_t = np.tanh(a[:, 2 * H:3 * H])
    o_t = sigmoid(a[:, 3 * H:4 * H])
    c_t = f_t * c0f + i_t * g_t
    th = np.tanh(c_t)
    go = f64(grad_out)
    gh, gc = go[0], go[1]
    dc = gc + gh * o_t * (1.0 - th * th)
    da = np.concatenate([dc * g_t * i_t * (1.0 - i_t),
                         dc * c0f * f_t * (1.0 - f_t),
                         dc * i_t * (1.0 - g_t * g_t),
                         gh * th * o_t * (1.0 - o_t)], axis=1)
    Wx = np.concatenate([f64(W_ii), f64(W_if), f64(W_ig), f64(W_io)], axis=0)
    return mxq(da, 1, "e5m2") @ mxq(Wx, 0, "e4m3")

@@ -1,0 +1,251 @@
+from contextlib import ExitStack
+
+import concourse.mybir as mybir
+from concourse.masks import make_identity
+
+F32 = mybir.dt.float32
+BF16 = mybir.dt.bfloat16
+U32 = mybir.dt.uint32
+U8 = mybir.dt.uint8
+E5M2_X4 = mybir.dt.float8_e5m2_x4
+E4M3_X4 = mybir.dt.float8_e4m3fn_x4
+FUNC = mybir.ActivationFunctionType
+ALU = mybir.AluOpType
+
+P = 128
+B, D, H = 2048, 1024, 256
+N_TILES = B // P
+HALVES = H // P
+PACK = 4
+PASSES = 4 * H // (P * PACK)
+N_COLS = 512
+N_BANKS = D // N_COLS
+RUN = 4
+SMALL_GROUP = 4
+W_CHUNK = 256
+
+FLOPS = 2 * B * D * 4 * H
+BYTES = 4 * B * 4 * H + 2 * B * H + 2 * 2 * B * H + 2 * 4 * H * D + 4 * B * D
+
+
+def tile_lstmcell_t_v_kernel(
+    tc, x, h0, c0,
+    W_ii, b_ii, W_hi, b_hi,
+    W_if, b_if, W_hf, b_hf,
+    W_ig, b_ig, W_hg, b_hg,
+    W_io, b_io, W_ho, b_ho,
+    gates, grad_out, out,
+):
+    nc = tc.nc
+
+    gates_rows = gates.rearrange("(p r) k -> p r k", r=N_TILES)
+    c0_rows = c0.rearrange("(p r) h -> p r h", r=N_TILES)
+    gh_rows = grad_out[0].rearrange("(p r) h -> p r h", r=N_TILES)
+    gc_rows = grad_out[1].rearrange("(p r) h -> p r h", r=N_TILES)
+    out_rows = out.rearrange("(p r) d -> p r d", r=N_TILES)
+
+    col_i, col_f, col_g, col_o = 0, H, 2 * H, 3 * H
+
+    with ExitStack() as stack:
+        consts = stack.enter_context(tc.tile_pool(name="consts", bufs=1))
+        resident = stack.enter_context(tc.tile_pool(name="resident", bufs=1))
+        gates_pool = stack.enter_context(tc.tile_pool(name="gates_pool", bufs=N_TILES))
+        work = stack.enter_context(tc.tile_pool(name="work", bufs=2))
+        out_pool = stack.enter_context(tc.tile_pool(name="out_pool", bufs=3))
+        psum_gates = stack.enter_context(tc.psum_pool(name="psum_gates", bufs=2))
+        psum_saved = stack.enter_context(tc.psum_pool(name="psum_saved", bufs=2))
+        psum_out = stack.enter_context(tc.psum_pool(name="psum_out", bufs=N_BANKS))
+        stack.enter_context(tc.manual_schedule())
+
+        ident_f32 = consts.tile([P, P], F32)
+        make_identity(nc, ident_f32[:])
+        ident_bf16 = consts.tile([P, P], BF16)
+        make_identity(nc, ident_bf16[:])
+
+        table_in = consts.tile([P, 1], F32)
+        table_out = consts.tile([P, 1], F32)
+        nc.vector.memset(table_in[:], 0.0)
+        nc.scalar.activation(out=table_out[:], in_=table_in[:], func=FUNC.Sigmoid)
+
+        w_raw = resident.tile([P, PASSES, PACK, D], BF16)
+        for q, pair in enumerate(((W_if, W_ii), (W_io, W_ig))):
+            for slot, w_gate in enumerate(pair):
+                nc.sync.dma_start(
+                    out=w_raw[:, q, HALVES * slot : HALVES * (slot + 1), :],
+                    in_=w_gate.rearrange("(c p) d -> p c d", p=P),
+                )
+
+        c0_sb = resident.tile([P, N_TILES, H], BF16)
+        gh_sb = resident.tile([P, N_TILES, H], BF16)
+        gc_sb = resident.tile([P, N_TILES, H], BF16)
+        gates_sb = []
+        for first in range(0, N_TILES, SMALL_GROUP):
+            group = slice(first, first + SMALL_GROUP)
+            for r in range(first, first + SMALL_GROUP):
+                gates_tile = gates_pool.tile([P, 4 * H], F32)
+                nc.sync.dma_start(out=gates_tile[:], in_=gates_rows[:, r, :])
+                gates_sb.append(gates_tile)
+                if r == first:
+                    nc.sync.dma_start(out=c0_sb[:, group, :], in_=c0_rows[:, group, :])
+                    nc.sync.dma_start(out=gh_sb[:, group, :], in_=gh_rows[:, group, :])
+                    nc.sync.dma_start(out=gc_sb[:, group, :], in_=gc_rows[:, group, :])
+
+        w_grouped = resident.tile([P, PASSES, D, PACK], BF16, align_bytes=64)
+        w_codes = resident.tile([P, PASSES, D], U32, align_bytes=64)
+        w_scales = resident.tile([P, PASSES, D], U8, align_bytes=64)
+        chunk = 0
+        for q in range(PASSES):
+            for d0 in range(0, D, W_CHUNK):
+                dst = w_grouped[:, q, d0 : d0 + W_CHUNK, :].rearrange("p (b i) t -> p b t i", i=RUN)
+                src = w_raw[:, q, :, d0 : d0 + W_CHUNK].rearrange("p t (b i) -> p b t i", i=RUN)
+                if chunk % 3 == 2:
+                    nc.scalar.copy(out=dst, in_=src)
+                else:
+                    nc.vector.tensor_copy(out=dst, in_=src)
+                chunk += 1
+        for q in range(PASSES):
+            nc.vector.quantize_mx(
+                out=w_codes[:, q, :].bitcast(E4M3_X4),
+                scales=w_scales[:, q, :],
+                in_=w_grouped[:, q].rearrange("p d t -> p (d t)"),
+            )
+
+        tiles = {}
+
+        def transpose_gates(n):
+            pre_fi = psum_gates.tile([P, 2, HALVES, P], F32)
+            pre_og = psum_gates.tile([P, 2, HALVES, P], F32)
+            for bank, cols in ((pre_fi, (col_f, col_i)), (pre_og, (col_o, col_g))):
+                for slot, col in enumerate(cols):
+                    for c in range(HALVES):
+                        nc.tensor.transpose(
+                            bank[:, slot, c, :], gates_sb[n][:, col + c * P : col + (c + 1) * P], ident_f32[:]
+                        )
+            tiles["pre_fi", n] = pre_fi
+            tiles["pre_og", n] = pre_og
+
+        def transpose_saved(n):
+            saved = psum_saved.tile([P, 3, HALVES, P], BF16)
+            for slot, rows in enumerate((c0_sb, gh_sb, gc_sb)):
+                for c in range(HALVES):
+                    nc.tensor.transpose(saved[:, slot, c, :], rows[:, n, c * P : (c + 1) * P], ident_bf16[:])
+            tiles["saved", n] = saved
+
+        def gate_activations(n):
+            sigm = work.tile([P, 3, HALVES, P], F32)
+            g = work.tile([P, HALVES, P], F32)
+            g_sq = work.tile([P, HALVES, P], F32)
+            nc.scalar.activation(out=sigm[:, 0:2], in_=tiles["pre_fi", n][:], func=FUNC.Sigmoid)
+            nc.scalar.activation(out=sigm[:, 2], in_=tiles["pre_og", n][:, 0], func=FUNC.Sigmoid)
+            nc.scalar.activation(out=g[:], in_=tiles["pre_og", n][:, 1], func=FUNC.Tanh)
+            nc.scalar.activation(out=g_sq[:], in_=g[:], func=FUNC.Square)
+            tiles["sigm", n], tiles["g", n], tiles["g_sq", n] = sigm, g, g_sq
+
+        def products(n):
+            prod = work.tile([P, 3, HALVES, P], F32)
+            sigm = tiles["sigm", n]
+            nc.vector.tensor_tensor(out=prod[:, 0::2], in0=sigm[:, 0::2], in1=tiles["saved", n][:, 0:2], op=ALU.mult)
+            nc.vector.tensor_tensor(out=prod[:, 1], in0=sigm[:, 1], in1=tiles["g", n][:], op=ALU.mult)
+            tiles["prod", n] = prod
+
+        def cell_state(n):
+            cell = work.tile([P, HALVES, P], F32)
+            prod = tiles["prod", n]
+            nc.vector.tensor_tensor(out=cell[:], in0=prod[:, 0], in1=prod[:, 1], op=ALU.add)
+            tiles["cell", n] = cell
+
+        def cell_tanh(n):
+            mult = work.tile([P, 3, HALVES, P], F32)
+            th_sq = work.tile([P, HALVES, P], F32)
+            nc.scalar.activation(out=mult[:, 0], in_=tiles["cell", n][:], func=FUNC.Tanh, scale=-1.0)
+            nc.scalar.activation(out=th_sq[:], in_=mult[:, 0], func=FUNC.Square)
+            tiles["mult", n], tiles["th_sq", n] = mult, th_sq
+
+        def factors(n):
+            factor = work.tile([P, 4, HALVES, P], F32)
+            sigm = tiles["sigm", n]
+            nc.vector.scalar_tensor_tensor(
+                out=factor[:, 0:3], in0=sigm[:], scalar=-1.0, in1=tiles["prod", n][:], op0=ALU.add, op1=ALU.mult
+            )
+            nc.vector.scalar_tensor_tensor(
+                out=factor[:, 3], in0=tiles["g_sq", n][:], scalar=-1.0, in1=sigm[:, 1], op0=ALU.add, op1=ALU.mult
+            )
+            tiles["factor", n] = factor
+
+        def through_tanh(n):
+            via_h = work.tile([P, HALVES, P], F32)
+            nc.vector.scalar_tensor_tensor(
+                out=via_h[:], in0=tiles["th_sq", n][:], scalar=-1.0, in1=tiles["prod", n][:, 2],
+                op0=ALU.add, op1=ALU.mult,
+            )
+            tiles["via_h", n] = via_h
+
+        def cell_gradient(n):
+            mult = tiles["mult", n]
+            nc.vector.tensor_tensor(out=mult[:, 1], in0=tiles["via_h", n][:], in1=tiles["saved", n][:, 2], op=ALU.subtract)
+            nc.scalar.copy(out=mult[:, 2], in_=mult[:, 1])
+
+        def gate_gradients(n):
+            da_grouped = work.tile([P, PASSES, P, PACK], BF16, align_bytes=64)
+            factor, mult = tiles["factor", n], tiles["mult", n]
+            for q, first_mult in ((1, 0), (0, 1)):
+                nc.vector.tensor_tensor(
+                    out=da_grouped[:, q].rearrange("p (b i) t -> p b t i", i=RUN),
+                    in0=factor[:, 2 * q : 2 * q + 2].rearrange("p s c n -> p (s c) n").rearrange("p t (b i) -> p b t i", i=RUN),
+                    in1=mult[:, first_mult : first_mult + 2].rearrange("p s c n -> p (s c) n").rearrange("p t (b i) -> p b t i", i=RUN),
+                    op=ALU.mult,
+                )
+            tiles["da_grouped", n] = da_grouped
+
+        def quantise(n):
+            da_codes = work.tile([P, PASSES * P], U32, align_bytes=64)
+            da_scales = work.tile([P, PASSES * P], U8, align_bytes=64)
+            nc.vector.quantize_mx(
+                out=da_codes[:].bitcast(E5M2_X4),
+                scales=da_scales[:],
+                in_=tiles["da_grouped", n][:].rearrange("p q n t -> p (q n t)"),
+            )
+            tiles["da_codes", n], tiles["da_scales", n] = da_codes, da_scales
+
+        def multiply(n):
+            da_codes, da_scales = tiles["da_codes", n], tiles["da_scales", n]
+            for bank in range(N_BANKS):
+                acc = psum_out.tile([P, N_COLS], F32)
+                cols = slice(bank * N_COLS, (bank + 1) * N_COLS)
+                for q in range(PASSES):
+                    toks = slice(q * P, (q + 1) * P)
+                    nc.tensor.matmul_mx(
+                        out=acc[:],
+                        lhsT=da_codes[:, toks].bitcast(E5M2_X4),
+                        lhsT_scale=da_scales[:, toks],
+                        rhs=w_codes[:, q, cols].bitcast(E4M3_X4),
+                        rhs_scale=w_scales[:, q, cols],
+                        start=(q == 0),
+                        stop=(q == PASSES - 1),
+                    )
+                tiles["acc", n, bank] = acc
+
+        def empty_and_store(n):
+            out_sb = out_pool.tile([P, D], F32)
+            for bank in range(N_BANKS):
+                nc.scalar.copy(out=out_sb[:, bank * N_COLS : (bank + 1) * N_COLS], in_=tiles["acc", n, bank][:])
+            nc.sync.dma_start(out=out_rows[:, n, :], in_=out_sb[:])
+
+        def run(stage, n):
+            if 0 <= n < N_TILES:
+                stage(n)
+
+        for n in range(-2, N_TILES + 3):
+            run(transpose_gates, n + 2)
+            run(empty_and_store, n - 3)
+            run(gate_activations, n + 1)
+            run(products, n)
+            run(quantise, n - 2)
+            run(multiply, n - 2)
+            run(through_tanh, n - 1)
+            run(cell_state, n)
+            run(cell_gradient, n - 1)
+            run(transpose_saved, n + 1)
+            run(cell_tanh, n)
+            run(factors, n)
+            run(gate_gradients, n - 1)

@@ -51,9 +51,10 @@ def tile_lstmcell_t_v_kernel(
         resident = stack.enter_context(tc.tile_pool(name="resident", bufs=1))
         gates_pool = stack.enter_context(tc.tile_pool(name="gates_pool", bufs=N_TILES))
         work = stack.enter_context(tc.tile_pool(name="work", bufs=2))
-        out_pool = stack.enter_context(tc.tile_pool(name="out_pool", bufs=3))
-        psum_gates = stack.enter_context(tc.psum_pool(name="psum_gates", bufs=2))
+        out_pool = stack.enter_context(tc.tile_pool(name="out_pool", bufs=3 * N_BANKS))
+        psum_gates = stack.enter_context(tc.psum_pool(name="psum_gates", bufs=3))
         psum_saved = stack.enter_context(tc.psum_pool(name="psum_saved", bufs=2))
+        psum_cell = stack.enter_context(tc.psum_pool(name="psum_cell", bufs=1))
         psum_out = stack.enter_context(tc.psum_pool(name="psum_out", bufs=N_BANKS))
         stack.enter_context(tc.manual_schedule())
 
@@ -113,8 +114,8 @@ def tile_lstmcell_t_v_kernel(
         tiles = {}
 
         def transpose_gates(n):
-            pre_fi = psum_gates.tile([P, 2, HALVES, P], F32)
-            pre_og = psum_gates.tile([P, 2, HALVES, P], F32)
+            pre_fi = psum_gates.tile([P, 2, HALVES, P], F32, tag="pre")
+            pre_og = psum_gates.tile([P, 2, HALVES, P], F32, tag="pre")
             for bank, cols in ((pre_fi, (col_f, col_i)), (pre_og, (col_o, col_g))):
                 for slot, col in enumerate(cols):
                     for c in range(HALVES):
@@ -149,9 +150,10 @@ def tile_lstmcell_t_v_kernel(
             tiles["prod", n] = prod
 
         def cell_state(n):
-            cell = work.tile([P, HALVES, P], F32)
+            cell = psum_cell.tile([P, HALVES, P], F32)
             prod = tiles["prod", n]
-            nc.vector.tensor_tensor(out=cell[:], in0=prod[:, 0], in1=prod[:, 1], op=ALU.add)
+            nc.tensor.matmul(out=cell[:], lhsT=ident_f32[:], rhs=prod[:, 0], start=True, stop=False)
+            nc.tensor.matmul(out=cell[:], lhsT=ident_f32[:], rhs=prod[:, 1], start=False, stop=True)
             tiles["cell", n] = cell
 
         def cell_tanh(n):
@@ -226,26 +228,29 @@ def tile_lstmcell_t_v_kernel(
                 tiles["acc", n, bank] = acc
 
         def empty_and_store(n):
-            out_sb = out_pool.tile([P, D], F32)
             for bank in range(N_BANKS):
-                nc.scalar.copy(out=out_sb[:, bank * N_COLS : (bank + 1) * N_COLS], in_=tiles["acc", n, bank][:])
-            nc.sync.dma_start(out=out_rows[:, n, :], in_=out_sb[:])
+                out_sb = out_pool.tile([P, N_COLS], F32)
+                if n == N_TILES - 1 and bank == N_BANKS - 1:
+                    nc.vector.tensor_copy(out=out_sb[:], in_=tiles["acc", n, bank][:])
+                else:
+                    nc.scalar.copy(out=out_sb[:], in_=tiles["acc", n, bank][:])
+                nc.sync.dma_start(out=out_rows[:, n, bank * N_COLS : (bank + 1) * N_COLS], in_=out_sb[:])
 
         def run(stage, n):
             if 0 <= n < N_TILES:
                 stage(n)
 
         for n in range(-2, N_TILES + 3):
-            run(transpose_gates, n + 2)
             run(empty_and_store, n - 3)
             run(gate_activations, n + 1)
-            run(products, n)
-            run(quantise, n - 2)
-            run(multiply, n - 2)
             run(through_tanh, n - 1)
+            run(products, n)
             run(cell_state, n)
             run(cell_gradient, n - 1)
-            run(transpose_saved, n + 1)
             run(cell_tanh, n)
+            run(quantise, n - 2)
+            run(multiply, n - 2)
             run(factors, n)
             run(gate_gradients, n - 1)
+            run(transpose_saved, n + 1)
+            run(transpose_gates, n + 2)

@@ -248,9 +248,9 @@ def tile_lstmcell_t_v_kernel(
             run(cell_state, n)
             run(cell_gradient, n - 1)
             run(cell_tanh, n)
+            run(transpose_saved, n + 1)
             run(quantise, n - 2)
             run(multiply, n - 2)
             run(factors, n)
             run(gate_gradients, n - 1)
-            run(transpose_saved, n + 1)
             run(transpose_gates, n + 2)

@@ -132,21 +132,24 @@ def tile_lstmcell_t_v_kernel(
                     nc.tensor.transpose(saved[:, slot, c, :], rows[:, n, c * P : (c + 1) * P], ident_bf16[:])
             tiles["saved", n] = saved
 
-        def gate_activations(n):
+        def gate_sigmoids(n):
             sigm = work.tile([P, 3, HALVES, P], F32)
-            g = work.tile([P, HALVES, P], F32)
-            g_sq = work.tile([P, HALVES, P], F32)
             nc.scalar.activation(out=sigm[:, 0:2], in_=tiles["pre_fi", n][:], func=FUNC.Sigmoid)
             nc.scalar.activation(out=sigm[:, 2], in_=tiles["pre_og", n][:, 0], func=FUNC.Sigmoid)
+            tiles["sigm", n] = sigm
+
+        def gate_tanh(n):
+            g = work.tile([P, HALVES, P], F32)
+            g_sq = work.tile([P, HALVES, P], F32)
             nc.scalar.activation(out=g[:], in_=tiles["pre_og", n][:, 1], func=FUNC.Tanh)
             nc.scalar.activation(out=g_sq[:], in_=g[:], func=FUNC.Square)
-            tiles["sigm", n], tiles["g", n], tiles["g_sq", n] = sigm, g, g_sq
+            tiles["g", n], tiles["g_sq", n] = g, g_sq
 
         def products(n):
             prod = work.tile([P, 3, HALVES, P], F32)
             sigm = tiles["sigm", n]
             nc.vector.tensor_tensor(out=prod[:, 0::2], in0=sigm[:, 0::2], in1=tiles["saved", n][:, 0:2], op=ALU.mult)
-            nc.vector.tensor_tensor(out=prod[:, 1], in0=sigm[:, 1], in1=tiles["g", n][:], op=ALU.mult)
+            nc.gpsimd.tensor_tensor(out=prod[:, 1], in0=sigm[:, 1], in1=tiles["g", n][:], op=ALU.mult)
             tiles["prod", n] = prod
 
         def cell_state(n):
@@ -242,12 +245,13 @@ def tile_lstmcell_t_v_kernel(
 
         for n in range(-2, N_TILES + 3):
             run(empty_and_store, n - 3)
-            run(gate_activations, n + 1)
+            run(gate_sigmoids, n + 1)
             run(through_tanh, n - 1)
             run(products, n)
             run(cell_state, n)
             run(cell_gradient, n - 1)
             run(cell_tanh, n)
+            run(gate_tanh, n + 1)
             run(transpose_saved, n + 1)
             run(quantise, n - 2)
             run(multiply, n - 2)

@@ -44,18 +44,21 @@ def tile_lstmcell_t_v_kernel(
     gc_rows = grad_out[1].rearrange("(p r) h -> p r h", r=N_TILES)
     out_rows = out.rearrange("(p r) d -> p r d", r=N_TILES)
 
-    col_i, col_f, col_g, col_o = 0, H, 2 * H, 3 * H
+    col_i, col_g, col_o = 0, 2 * H, 3 * H
 
     with ExitStack() as stack:
         consts = stack.enter_context(tc.tile_pool(name="consts", bufs=1))
         resident = stack.enter_context(tc.tile_pool(name="resident", bufs=1))
         gates_pool = stack.enter_context(tc.tile_pool(name="gates_pool", bufs=N_TILES))
+        ahead = stack.enter_context(tc.tile_pool(name="ahead", bufs=3))
+        natural = stack.enter_context(tc.tile_pool(name="natural", bufs=2))
         work = stack.enter_context(tc.tile_pool(name="work", bufs=2))
         out_pool = stack.enter_context(tc.tile_pool(name="out_pool", bufs=3 * N_BANKS))
-        psum_gates = stack.enter_context(tc.psum_pool(name="psum_gates", bufs=3))
-        psum_saved = stack.enter_context(tc.psum_pool(name="psum_saved", bufs=2))
+        psum_factor = stack.enter_context(tc.psum_pool(name="psum_factor", bufs=PASSES))
         psum_cell = stack.enter_context(tc.psum_pool(name="psum_cell", bufs=1))
-        psum_out = stack.enter_context(tc.psum_pool(name="psum_out", bufs=N_BANKS))
+        psum_ogh = stack.enter_context(tc.psum_pool(name="psum_ogh", bufs=1))
+        psum_gc = stack.enter_context(tc.psum_pool(name="psum_gc", bufs=1))
+        psum_out = stack.enter_context(tc.psum_pool(name="psum_out", bufs=3))
         stack.enter_context(tc.manual_schedule())
 
         ident_f32 = consts.tile([P, P], F32)
@@ -69,15 +72,14 @@ def tile_lstmcell_t_v_kernel(
         nc.scalar.activation(out=table_out[:], in_=table_in[:], func=FUNC.Sigmoid)
 
         w_raw = resident.tile([P, PASSES, PACK, D], BF16)
-        for q, pair in enumerate(((W_if, W_ii), (W_io, W_ig))):
+        for q, pair in enumerate(((W_ii, W_if), (W_io, W_ig))):
             for slot, w_gate in enumerate(pair):
                 nc.sync.dma_start(
                     out=w_raw[:, q, HALVES * slot : HALVES * (slot + 1), :],
                     in_=w_gate.rearrange("(c p) d -> p c d", p=P),
                 )
 
-        c0_sb = resident.tile([P, N_TILES, H], BF16)
-        gh_sb = resident.tile([P, N_TILES, H], BF16)
+        saved_sb = resident.tile([P, 2, N_TILES, H], BF16)
         gc_sb = resident.tile([P, N_TILES, H], BF16)
         gates_sb = []
         for first in range(0, N_TILES, SMALL_GROUP):
@@ -87,8 +89,8 @@ def tile_lstmcell_t_v_kernel(
                 nc.sync.dma_start(out=gates_tile[:], in_=gates_rows[:, r, :])
                 gates_sb.append(gates_tile)
                 if r == first:
-                    nc.sync.dma_start(out=c0_sb[:, group, :], in_=c0_rows[:, group, :])
-                    nc.sync.dma_start(out=gh_sb[:, group, :], in_=gh_rows[:, group, :])
+                    nc.sync.dma_start(out=saved_sb[:, 0, group, :], in_=c0_rows[:, group, :])
+                    nc.sync.dma_start(out=saved_sb[:, 1, group, :], in_=gh_rows[:, group, :])
                     nc.sync.dma_start(out=gc_sb[:, group, :], in_=gc_rows[:, group, :])
 
         w_grouped = resident.tile([P, PASSES, D, PACK], BF16, align_bytes=64)
@@ -113,94 +115,98 @@ def tile_lstmcell_t_v_kernel(
 
         tiles = {}
 
-        def transpose_gates(n):
-            pre_fi = psum_gates.tile([P, 2, HALVES, P], F32, tag="pre")
-            pre_og = psum_gates.tile([P, 2, HALVES, P], F32, tag="pre")
-            for bank, cols in ((pre_fi, (col_f, col_i)), (pre_og, (col_o, col_g))):
-                for slot, col in enumerate(cols):
-                    for c in range(HALVES):
-                        nc.tensor.transpose(
-                            bank[:, slot, c, :], gates_sb[n][:, col + c * P : col + (c + 1) * P], ident_f32[:]
-                        )
-            tiles["pre_fi", n] = pre_fi
-            tiles["pre_og", n] = pre_og
-
-        def transpose_saved(n):
-            saved = psum_saved.tile([P, 3, HALVES, P], BF16)
-            for slot, rows in enumerate((c0_sb, gh_sb, gc_sb)):
-                for c in range(HALVES):
-                    nc.tensor.transpose(saved[:, slot, c, :], rows[:, n, c * P : (c + 1) * P], ident_bf16[:])
-            tiles["saved", n] = saved
-
-        def gate_sigmoids(n):
-            sigm = work.tile([P, 3, HALVES, P], F32)
-            nc.scalar.activation(out=sigm[:, 0:2], in_=tiles["pre_fi", n][:], func=FUNC.Sigmoid)
-            nc.scalar.activation(out=sigm[:, 2], in_=tiles["pre_og", n][:, 0], func=FUNC.Sigmoid)
-            tiles["sigm", n] = sigm
-
-        def gate_tanh(n):
-            g = work.tile([P, HALVES, P], F32)
-            g_sq = work.tile([P, HALVES, P], F32)
-            nc.scalar.activation(out=g[:], in_=tiles["pre_og", n][:, 1], func=FUNC.Tanh)
-            nc.scalar.activation(out=g_sq[:], in_=g[:], func=FUNC.Square)
-            tiles["g", n], tiles["g_sq", n] = g, g_sq
+        def activations(n):
+            act = ahead.tile([P, 4, H], F32)
+            g_sq = ahead.tile([P, H], F32)
+            pre = gates_sb[n]
+            nc.scalar.activation(out=act[:, 0:2], in_=pre[:, col_i : col_i + 2 * H].rearrange("p (s h) -> p s h", s=2), func=FUNC.Sigmoid)
+            nc.scalar.activation(out=act[:, 3], in_=pre[:, col_g : col_g + H], func=FUNC.Tanh)
+            nc.scalar.activation(out=act[:, 2], in_=pre[:, col_o : col_o + H], func=FUNC.Sigmoid)
+            nc.scalar.activation(out=g_sq[:], in_=act[:, 3], func=FUNC.Square)
+            tiles["act", n], tiles["g_sq", n] = act, g_sq
 
         def products(n):
-            prod = work.tile([P, 3, HALVES, P], F32)
-            sigm = tiles["sigm", n]
-            nc.vector.tensor_tensor(out=prod[:, 0::2], in0=sigm[:, 0::2], in1=tiles["saved", n][:, 0:2], op=ALU.mult)
-            nc.gpsimd.tensor_tensor(out=prod[:, 1], in0=sigm[:, 1], in1=tiles["g", n][:], op=ALU.mult)
+            prod = natural.tile([P, 3, H], F32)
+            act = tiles["act", n]
+            nc.gpsimd.tensor_tensor(out=prod[:, 0], in0=act[:, 0], in1=act[:, 3], op=ALU.mult)
+            nc.gpsimd.tensor_tensor(out=prod[:, 1:3], in0=act[:, 1:3], in1=saved_sb[:, :, n, :], op=ALU.mult)
             tiles["prod", n] = prod
 
-        def cell_state(n):
-            cell = psum_cell.tile([P, HALVES, P], F32)
+        def sigmoid_factors(n):
+            factor = natural.tile([P, 4, H], F32)
+            nc.vector.scalar_tensor_tensor(
+                out=factor[:, 0:3], in0=tiles["act", n][:, 0:3], scalar=-1.0, in1=tiles["prod", n][:],
+                op0=ALU.add, op1=ALU.mult,
+            )
+            tiles["factor", n] = factor
+
+        def tanh_factor(n):
+            nc.vector.scalar_tensor_tensor(
+                out=tiles["factor", n][:, 3], in0=tiles["g_sq", n][:], scalar=-1.0, in1=tiles["act", n][:, 0],
+                op0=ALU.add, op1=ALU.mult,
+            )
+
+        def transpose_cell(n):
             prod = tiles["prod", n]
-            nc.tensor.matmul(out=cell[:], lhsT=ident_f32[:], rhs=prod[:, 0], start=True, stop=False)
-            nc.tensor.matmul(out=cell[:], lhsT=ident_f32[:], rhs=prod[:, 1], start=False, stop=True)
-            tiles["cell", n] = cell
+            cell = psum_cell.tile([P, HALVES, P], F32)
+            for c in range(HALVES):
+                cols = slice(c * P, (c + 1) * P)
+                nc.tensor.matmul(out=cell[:, c, :], lhsT=prod[:, 0, cols], rhs=ident_f32[:], is_transpose=True, start=True, stop=False)
+                nc.tensor.matmul(out=cell[:, c, :], lhsT=prod[:, 1, cols], rhs=ident_f32[:], is_transpose=True, start=False, stop=True)
+            ogh = psum_ogh.tile([P, HALVES, P], F32)
+            gc = psum_gc.tile([P, HALVES, P], BF16)
+            for c in range(HALVES):
+                cols = slice(c * P, (c + 1) * P)
+                nc.tensor.transpose(ogh[:, c, :], prod[:, 2, cols], ident_f32[:])
+            for c in range(HALVES):
+                cols = slice(c * P, (c + 1) * P)
+                nc.tensor.transpose(gc[:, c, :], gc_sb[:, n, cols], ident_bf16[:])
+            tiles["cell", n], tiles["ogh", n], tiles["gc", n] = cell, ogh, gc
+
+        def transpose_factors(n):
+            factor = tiles["factor", n]
+            for q in range(PASSES):
+                bank = psum_factor.tile([P, PACK, P], F32, tag="factor_t")
+                for slot in range(2):
+                    for c in range(HALVES):
+                        nc.tensor.transpose(
+                            bank[:, HALVES * slot + c, :], factor[:, 2 * q + slot, c * P : (c + 1) * P], ident_f32[:]
+                        )
+                tiles["factor_t", n, q] = bank
 
         def cell_tanh(n):
-            mult = work.tile([P, 3, HALVES, P], F32)
+            mult = ahead.tile([P, 2, HALVES, P], F32)
             th_sq = work.tile([P, HALVES, P], F32)
             nc.scalar.activation(out=mult[:, 0], in_=tiles["cell", n][:], func=FUNC.Tanh, scale=-1.0)
             nc.scalar.activation(out=th_sq[:], in_=mult[:, 0], func=FUNC.Square)
             tiles["mult", n], tiles["th_sq", n] = mult, th_sq
 
-        def factors(n):
-            factor = work.tile([P, 4, HALVES, P], F32)
-            sigm = tiles["sigm", n]
-            nc.vector.scalar_tensor_tensor(
-                out=factor[:, 0:3], in0=sigm[:], scalar=-1.0, in1=tiles["prod", n][:], op0=ALU.add, op1=ALU.mult
-            )
-            nc.vector.scalar_tensor_tensor(
-                out=factor[:, 3], in0=tiles["g_sq", n][:], scalar=-1.0, in1=sigm[:, 1], op0=ALU.add, op1=ALU.mult
-            )
-            tiles["factor", n] = factor
-
         def through_tanh(n):
             via_h = work.tile([P, HALVES, P], F32)
             nc.vector.scalar_tensor_tensor(
-                out=via_h[:], in0=tiles["th_sq", n][:], scalar=-1.0, in1=tiles["prod", n][:, 2],
+                out=via_h[:], in0=tiles["th_sq", n][:], scalar=-1.0, in1=tiles["ogh", n][:],
                 op0=ALU.add, op1=ALU.mult,
             )
             tiles["via_h", n] = via_h
 
         def cell_gradient(n):
-            mult = tiles["mult", n]
-            nc.vector.tensor_tensor(out=mult[:, 1], in0=tiles["via_h", n][:], in1=tiles["saved", n][:, 2], op=ALU.subtract)
-            nc.scalar.copy(out=mult[:, 2], in_=mult[:, 1])
+            nc.vector.tensor_tensor(out=tiles["mult", n][:, 1], in0=tiles["via_h", n][:], in1=tiles["gc", n][:], op=ALU.subtract)
 
-        def gate_gradients(n):
-            da_grouped = work.tile([P, PASSES, P, PACK], BF16, align_bytes=64)
-            factor, mult = tiles["factor", n], tiles["mult", n]
-            for q, first_mult in ((1, 0), (0, 1)):
-                nc.vector.tensor_tensor(
-                    out=da_grouped[:, q].rearrange("p (b i) t -> p b t i", i=RUN),
-                    in0=factor[:, 2 * q : 2 * q + 2].rearrange("p s c n -> p (s c) n").rearrange("p t (b i) -> p b t i", i=RUN),
-                    in1=mult[:, first_mult : first_mult + 2].rearrange("p s c n -> p (s c) n").rearrange("p t (b i) -> p b t i", i=RUN),
-                    op=ALU.mult,
-                )
-            tiles["da_grouped", n] = da_grouped
+        def gate_gradients(n, q):
+            if q == 0:
+                da_grouped = work.tile([P, PASSES, P, PACK], BF16, align_bytes=64)
+                tiles["da_grouped", n] = da_grouped
+            da_grouped, mult = tiles["da_grouped", n], tiles["mult", n]
+            if q == 0:
+                multiplier = mult[:, 1].rearrange("p c n -> p n c").unsqueeze(2).to_broadcast([P, P, 2, HALVES])
+            else:
+                multiplier = mult[:].rearrange("p s c n -> p n s c")
+            nc.vector.tensor_tensor(
+                out=da_grouped[:, q].rearrange("p n (s c) -> p n s c", s=2),
+                in0=tiles["factor_t", n, q][:].rearrange("p (s c) n -> p n s c", s=2),
+                in1=multiplier,
+                op=ALU.mult,
+            )
 
         def quantise(n):
             da_codes = work.tile([P, PASSES * P], U32, align_bytes=64)
@@ -230,31 +236,31 @@ def tile_lstmcell_t_v_kernel(
                     )
                 tiles["acc", n, bank] = acc
 
-        def empty_and_store(n):
-            for bank in range(N_BANKS):
-                out_sb = out_pool.tile([P, N_COLS], F32)
-                if n == N_TILES - 1 and bank == N_BANKS - 1:
-                    nc.vector.tensor_copy(out=out_sb[:], in_=tiles["acc", n, bank][:])
-                else:
-                    nc.scalar.copy(out=out_sb[:], in_=tiles["acc", n, bank][:])
-                nc.sync.dma_start(out=out_rows[:, n, bank * N_COLS : (bank + 1) * N_COLS], in_=out_sb[:])
+        def empty_and_store(n, bank):
+            out_sb = out_pool.tile([P, N_COLS], F32)
+            if n == N_TILES - 1 and bank == N_BANKS - 1:
+                nc.vector.tensor_copy(out=out_sb[:], in_=tiles["acc", n, bank][:])
+            else:
+                nc.scalar.copy(out=out_sb[:], in_=tiles["acc", n, bank][:])
+            nc.sync.dma_start(out=out_rows[:, n, bank * N_COLS : (bank + 1) * N_COLS], in_=out_sb[:])
 
-        def run(stage, n):
+        def run(stage, n, *more):
             if 0 <= n < N_TILES:
-                stage(n)
+                stage(n, *more)
 
-        for n in range(-2, N_TILES + 3):
-            run(empty_and_store, n - 3)
-            run(gate_sigmoids, n + 1)
-            run(through_tanh, n - 1)
-            run(products, n)
-            run(cell_state, n)
-            run(cell_gradient, n - 1)
-            run(cell_tanh, n)
-            run(gate_tanh, n + 1)
-            run(transpose_saved, n + 1)
-            run(quantise, n - 2)
-            run(multiply, n - 2)
-            run(factors, n)
-            run(gate_gradients, n - 1)
-            run(transpose_gates, n + 2)
+        for r in range(-3, N_TILES + 1):
+            run(activations, r + 3)
+            run(products, r + 2)
+            run(through_tanh, r + 1)
+            run(gate_gradients, r, 0)
+            run(cell_gradient, r + 1)
+            run(gate_gradients, r, 1)
+            run(empty_and_store, r - 1, 0)
+            run(transpose_cell, r + 2)
+            run(cell_tanh, r + 2)
+            run(empty_and_store, r - 1, 1)
+            run(sigmoid_factors, r + 1)
+            run(quantise, r)
+            run(tanh_factor, r + 1)
+            run(transpose_factors, r + 1)
+            run(multiply, r)

@@ -133,18 +133,18 @@ def tile_lstmcell_t_v_kernel(
             tiles["prod", n] = prod
 
         def sigmoid_factors(n):
+            nc.vector.scalar_tensor_tensor(
+                out=tiles["factor", n][:, 0:3], in0=tiles["act", n][:, 0:3], scalar=-1.0, in1=tiles["prod", n][:],
+                op0=ALU.add, op1=ALU.mult,
+            )
+
+        def tanh_factor(n):
             factor = natural.tile([P, 4, H], F32)
             nc.vector.scalar_tensor_tensor(
-                out=factor[:, 0:3], in0=tiles["act", n][:, 0:3], scalar=-1.0, in1=tiles["prod", n][:],
+                out=factor[:, 3], in0=tiles["g_sq", n][:], scalar=-1.0, in1=tiles["act", n][:, 0],
                 op0=ALU.add, op1=ALU.mult,
             )
             tiles["factor", n] = factor
-
-        def tanh_factor(n):
-            nc.vector.scalar_tensor_tensor(
-                out=tiles["factor", n][:, 3], in0=tiles["g_sq", n][:], scalar=-1.0, in1=tiles["act", n][:, 0],
-                op0=ALU.add, op1=ALU.mult,
-            )
 
         def transpose_cell(n):
             prod = tiles["prod", n]
@@ -153,26 +153,28 @@ def tile_lstmcell_t_v_kernel(
                 cols = slice(c * P, (c + 1) * P)
                 nc.tensor.matmul(out=cell[:, c, :], lhsT=prod[:, 0, cols], rhs=ident_f32[:], is_transpose=True, start=True, stop=False)
                 nc.tensor.matmul(out=cell[:, c, :], lhsT=prod[:, 1, cols], rhs=ident_f32[:], is_transpose=True, start=False, stop=True)
+            tiles["cell", n] = cell
+
+        def transpose_grads(n):
             ogh = psum_ogh.tile([P, HALVES, P], F32)
             gc = psum_gc.tile([P, HALVES, P], BF16)
             for c in range(HALVES):
                 cols = slice(c * P, (c + 1) * P)
-                nc.tensor.transpose(ogh[:, c, :], prod[:, 2, cols], ident_f32[:])
+                nc.tensor.transpose(ogh[:, c, :], tiles["prod", n][:, 2, cols], ident_f32[:])
             for c in range(HALVES):
                 cols = slice(c * P, (c + 1) * P)
                 nc.tensor.transpose(gc[:, c, :], gc_sb[:, n, cols], ident_bf16[:])
-            tiles["cell", n], tiles["ogh", n], tiles["gc", n] = cell, ogh, gc
+            tiles["ogh", n], tiles["gc", n] = ogh, gc
 
-        def transpose_factors(n):
+        def transpose_factors(n, q):
             factor = tiles["factor", n]
-            for q in range(PASSES):
-                bank = psum_factor.tile([P, PACK, P], F32, tag="factor_t")
-                for slot in range(2):
-                    for c in range(HALVES):
-                        nc.tensor.transpose(
-                            bank[:, HALVES * slot + c, :], factor[:, 2 * q + slot, c * P : (c + 1) * P], ident_f32[:]
-                        )
-                tiles["factor_t", n, q] = bank
+            bank = psum_factor.tile([P, PACK, P], F32, tag="factor_t")
+            for slot in range(2):
+                for c in range(HALVES):
+                    nc.tensor.transpose(
+                        bank[:, HALVES * slot + c, :], factor[:, 2 * q + slot, c * P : (c + 1) * P], ident_f32[:]
+                    )
+            tiles["factor_t", n, q] = bank
 
         def cell_tanh(n):
             mult = ahead.tile([P, 2, HALVES, P], F32)
@@ -193,7 +195,7 @@ def tile_lstmcell_t_v_kernel(
             nc.vector.tensor_tensor(out=tiles["mult", n][:, 1], in0=tiles["via_h", n][:], in1=tiles["gc", n][:], op=ALU.subtract)
 
         def gate_gradients(n, q):
-            if q == 0:
+            if q == 1:
                 da_grouped = work.tile([P, PASSES, P, PACK], BF16, align_bytes=64)
                 tiles["da_grouped", n] = da_grouped
             da_grouped, mult = tiles["da_grouped", n], tiles["mult", n]
@@ -248,19 +250,21 @@ def tile_lstmcell_t_v_kernel(
             if 0 <= n < N_TILES:
                 stage(n, *more)
 
-        for r in range(-3, N_TILES + 1):
-            run(activations, r + 3)
-            run(products, r + 2)
+        for r in range(-4, N_TILES + 1):
+            run(activations, r + 4)
+            run(products, r + 3)
             run(through_tanh, r + 1)
-            run(gate_gradients, r, 0)
-            run(cell_gradient, r + 1)
             run(gate_gradients, r, 1)
-            run(empty_and_store, r - 1, 0)
+            run(cell_gradient, r + 1)
+            run(gate_gradients, r, 0)
             run(transpose_cell, r + 2)
             run(cell_tanh, r + 2)
-            run(empty_and_store, r - 1, 1)
-            run(sigmoid_factors, r + 1)
+            run(transpose_factors, r + 1, 1)
+            run(transpose_grads, r + 2)
+            run(transpose_factors, r + 1, 0)
+            run(tanh_factor, r + 2)
             run(quantise, r)
-            run(tanh_factor, r + 1)
-            run(transpose_factors, r + 1)
+            run(sigmoid_factors, r + 2)
+            run(empty_and_store, r - 1, 0)
+            run(empty_and_store, r - 1, 1)
             run(multiply, r)

@@ -200,15 +200,19 @@ def tile_lstmcell_t_v_kernel(
                 tiles["da_grouped", n] = da_grouped
             da_grouped, mult = tiles["da_grouped", n], tiles["mult", n]
             if q == 0:
-                multiplier = mult[:, 1].rearrange("p c n -> p n c").unsqueeze(2).to_broadcast([P, P, 2, HALVES])
+                nc.vector.tensor_tensor(
+                    out=da_grouped[:, q].rearrange("p n (s c) -> p n s c", s=2),
+                    in0=tiles["factor_t", n, q][:].rearrange("p (s c) n -> p n s c", s=2),
+                    in1=mult[:, 1].rearrange("p c n -> p n c").unsqueeze(2).to_broadcast([P, P, 2, HALVES]),
+                    op=ALU.mult,
+                )
             else:
-                multiplier = mult[:].rearrange("p s c n -> p n s c")
-            nc.vector.tensor_tensor(
-                out=da_grouped[:, q].rearrange("p n (s c) -> p n s c", s=2),
-                in0=tiles["factor_t", n, q][:].rearrange("p (s c) n -> p n s c", s=2),
-                in1=multiplier,
-                op=ALU.mult,
-            )
+                nc.vector.tensor_tensor(
+                    out=da_grouped[:, q].rearrange("p (b i) t -> p b t i", i=RUN),
+                    in0=tiles["factor_t", n, q][:].rearrange("p t (b i) -> p b t i", i=RUN),
+                    in1=mult[:].rearrange("p s c n -> p (s c) n").rearrange("p t (b i) -> p b t i", i=RUN),
+                    op=ALU.mult,
+                )
 
         def quantise(n):
             da_codes = work.tile([P, PASSES * P], U32, align_bytes=64)

@@ -116,43 +116,43 @@ def tile_lstmcell_t_v_kernel(
         tiles = {}
 
         def activations(n):
-            act = ahead.tile([P, 4, H], F32)
-            g_sq = ahead.tile([P, H], F32)
+            nat = ahead.tile([P, 5, H], F32)
+            g = ahead.tile([P, H], F32)
             pre = gates_sb[n]
-            nc.scalar.activation(out=act[:, 0:2], in_=pre[:, col_i : col_i + 2 * H].rearrange("p (s h) -> p s h", s=2), func=FUNC.Sigmoid)
-            nc.scalar.activation(out=act[:, 3], in_=pre[:, col_g : col_g + H], func=FUNC.Tanh)
-            nc.scalar.activation(out=act[:, 2], in_=pre[:, col_o : col_o + H], func=FUNC.Sigmoid)
-            nc.scalar.activation(out=g_sq[:], in_=act[:, 3], func=FUNC.Square)
-            tiles["act", n], tiles["g_sq", n] = act, g_sq
+            nc.scalar.activation(out=nat[:, 1:4:2], in_=pre[:, col_i : col_i + 2 * H].rearrange("p (s h) -> p s h", s=2), func=FUNC.Sigmoid)
+            nc.scalar.activation(out=g[:], in_=pre[:, col_g : col_g + H], func=FUNC.Tanh)
+            nc.scalar.activation(out=nat[:, 4], in_=pre[:, col_o : col_o + H], func=FUNC.Sigmoid)
+            nc.scalar.activation(out=nat[:, 2], in_=g[:], func=FUNC.Square)
+            tiles["nat", n], tiles["g", n] = nat, g
 
         def products(n):
-            prod = natural.tile([P, 3, H], F32)
-            act = tiles["act", n]
-            nc.gpsimd.tensor_tensor(out=prod[:, 0], in0=act[:, 0], in1=act[:, 3], op=ALU.mult)
-            nc.gpsimd.tensor_tensor(out=prod[:, 1:3], in0=act[:, 1:3], in1=saved_sb[:, :, n, :], op=ALU.mult)
-            tiles["prod", n] = prod
+            prod_fo = natural.tile([P, 2, H], F32)
+            nat = tiles["nat", n]
+            nc.gpsimd.tensor_tensor(out=prod_fo[:], in0=nat[:, 3:5], in1=saved_sb[:, :, n, :], op=ALU.mult)
+            nc.gpsimd.tensor_tensor(out=nat[:, 0], in0=nat[:, 1], in1=tiles["g", n][:], op=ALU.mult)
+            tiles["prod_fo", n] = prod_fo
 
-        def sigmoid_factors(n):
-            nc.vector.scalar_tensor_tensor(
-                out=tiles["factor", n][:, 0:3], in0=tiles["act", n][:, 0:3], scalar=-1.0, in1=tiles["prod", n][:],
-                op0=ALU.add, op1=ALU.mult,
-            )
-
-        def tanh_factor(n):
+        def fo_factors(n):
             factor = natural.tile([P, 4, H], F32)
             nc.vector.scalar_tensor_tensor(
-                out=factor[:, 3], in0=tiles["g_sq", n][:], scalar=-1.0, in1=tiles["act", n][:, 0],
+                out=factor[:, 1:3], in0=tiles["nat", n][:, 3:5], scalar=-1.0, in1=tiles["prod_fo", n][:],
                 op0=ALU.add, op1=ALU.mult,
             )
             tiles["factor", n] = factor
 
+        def ig_factors(n):
+            nat = tiles["nat", n]
+            nc.vector.scalar_tensor_tensor(
+                out=tiles["factor", n][:, 0::3], in0=nat[:, 1:3], scalar=-1.0, in1=nat[:, 0:2],
+                op0=ALU.add, op1=ALU.mult,
+            )
+
         def transpose_cell(n):
-            prod = tiles["prod", n]
             cell = psum_cell.tile([P, HALVES, P], F32)
             for c in range(HALVES):
                 cols = slice(c * P, (c + 1) * P)
-                nc.tensor.matmul(out=cell[:, c, :], lhsT=prod[:, 0, cols], rhs=ident_f32[:], is_transpose=True, start=True, stop=False)
-                nc.tensor.matmul(out=cell[:, c, :], lhsT=prod[:, 1, cols], rhs=ident_f32[:], is_transpose=True, start=False, stop=True)
+                nc.tensor.matmul(out=cell[:, c, :], lhsT=tiles["prod_fo", n][:, 0, cols], rhs=ident_f32[:], is_transpose=True, start=True, stop=False)
+                nc.tensor.matmul(out=cell[:, c, :], lhsT=tiles["nat", n][:, 0, cols], rhs=ident_f32[:], is_transpose=True, start=False, stop=True)
             tiles["cell", n] = cell
 
         def transpose_grads(n):
@@ -160,7 +160,7 @@ def tile_lstmcell_t_v_kernel(
             gc = psum_gc.tile([P, HALVES, P], BF16)
             for c in range(HALVES):
                 cols = slice(c * P, (c + 1) * P)
-                nc.tensor.transpose(ogh[:, c, :], tiles["prod", n][:, 2, cols], ident_f32[:])
+                nc.tensor.transpose(ogh[:, c, :], tiles["prod_fo", n][:, 1, cols], ident_f32[:])
             for c in range(HALVES):
                 cols = slice(c * P, (c + 1) * P)
                 nc.tensor.transpose(gc[:, c, :], gc_sb[:, n, cols], ident_bf16[:])
@@ -259,16 +259,16 @@ def tile_lstmcell_t_v_kernel(
             run(products, r + 3)
             run(through_tanh, r + 1)
             run(gate_gradients, r, 1)
-            run(cell_gradient, r + 1)
             run(gate_gradients, r, 0)
+            run(cell_gradient, r + 1)
             run(transpose_cell, r + 2)
             run(cell_tanh, r + 2)
             run(transpose_factors, r + 1, 1)
-            run(transpose_grads, r + 2)
             run(transpose_factors, r + 1, 0)
-            run(tanh_factor, r + 2)
+            run(transpose_grads, r + 2)
             run(quantise, r)
-            run(sigmoid_factors, r + 2)
+            run(fo_factors, r + 2)
+            run(ig_factors, r + 2)
             run(empty_and_store, r - 1, 0)
             run(empty_and_store, r - 1, 1)
             run(multiply, r)

@@ -178,10 +178,13 @@ def tile_lstmcell_t_v_kernel(
 
         def cell_tanh(n):
             mult = ahead.tile([P, 2, HALVES, P], F32)
-            th_sq = work.tile([P, HALVES, P], F32)
             nc.scalar.activation(out=mult[:, 0], in_=tiles["cell", n][:], func=FUNC.Tanh, scale=-1.0)
-            nc.scalar.activation(out=th_sq[:], in_=mult[:, 0], func=FUNC.Square)
-            tiles["mult", n], tiles["th_sq", n] = mult, th_sq
+            tiles["mult", n] = mult
+
+        def cell_square(n):
+            th_sq = work.tile([P, HALVES, P], F32)
+            nc.scalar.activation(out=th_sq[:], in_=tiles["mult", n][:, 0], func=FUNC.Square)
+            tiles["th_sq", n] = th_sq
 
         def through_tanh(n):
             via_h = work.tile([P, HALVES, P], F32)
@@ -270,5 +273,6 @@ def tile_lstmcell_t_v_kernel(
             run(fo_factors, r + 2)
             run(ig_factors, r + 2)
             run(empty_and_store, r - 1, 0)
+            run(cell_square, r + 2)
             run(empty_and_store, r - 1, 1)
             run(multiply, r)

from contextlib import ExitStack

import concourse.mybir as mybir
from concourse.masks import make_identity

F32 = mybir.dt.float32
BF16 = mybir.dt.bfloat16
U32 = mybir.dt.uint32
U8 = mybir.dt.uint8
E5M2_X4 = mybir.dt.float8_e5m2_x4
E4M3_X4 = mybir.dt.float8_e4m3fn_x4
FUNC = mybir.ActivationFunctionType
ALU = mybir.AluOpType

P = 128
B, D, H = 2048, 1024, 256
N_TILES = B // P
HALVES = H // P
PACK = 4
PASSES = 4 * H // (P * PACK)
N_COLS = 512
N_BANKS = D // N_COLS
RUN = 4
SMALL_GROUP = 4
W_CHUNK = 256

FLOPS = 2 * B * D * 4 * H
BYTES = 4 * B * 4 * H + 2 * B * H + 2 * 2 * B * H + 2 * 4 * H * D + 4 * B * D


def tile_lstmcell_t_v_kernel(
    tc, x, h0, c0,
    W_ii, b_ii, W_hi, b_hi,
    W_if, b_if, W_hf, b_hf,
    W_ig, b_ig, W_hg, b_hg,
    W_io, b_io, W_ho, b_ho,
    gates, grad_out, out,
):
    nc = tc.nc

    gates_rows = gates.rearrange("(p r) k -> p r k", r=N_TILES)
    c0_rows = c0.rearrange("(p r) h -> p r h", r=N_TILES)
    gh_rows = grad_out[0].rearrange("(p r) h -> p r h", r=N_TILES)
    gc_rows = grad_out[1].rearrange("(p r) h -> p r h", r=N_TILES)
    out_rows = out.rearrange("(p r) d -> p r d", r=N_TILES)

    col_i, col_g, col_o = 0, 2 * H, 3 * H

    with ExitStack() as stack:
        consts = stack.enter_context(tc.tile_pool(name="consts", bufs=1))
        resident = stack.enter_context(tc.tile_pool(name="resident", bufs=1))
        gates_pool = stack.enter_context(tc.tile_pool(name="gates_pool", bufs=N_TILES))
        ahead = stack.enter_context(tc.tile_pool(name="ahead", bufs=3))
        natural = stack.enter_context(tc.tile_pool(name="natural", bufs=2))
        work = stack.enter_context(tc.tile_pool(name="work", bufs=2))
        out_pool = stack.enter_context(tc.tile_pool(name="out_pool", bufs=3 * N_BANKS))
        psum_factor = stack.enter_context(tc.psum_pool(name="psum_factor", bufs=PASSES))
        psum_cell = stack.enter_context(tc.psum_pool(name="psum_cell", bufs=1))
        psum_ogh = stack.enter_context(tc.psum_pool(name="psum_ogh", bufs=1))
        psum_gc = stack.enter_context(tc.psum_pool(name="psum_gc", bufs=1))
        psum_out = stack.enter_context(tc.psum_pool(name="psum_out", bufs=3))
        stack.enter_context(tc.manual_schedule())

        ident_f32 = consts.tile([P, P], F32)
        make_identity(nc, ident_f32[:])
        ident_bf16 = consts.tile([P, P], BF16)
        make_identity(nc, ident_bf16[:])

        table_in = consts.tile([P, 1], F32)
        table_out = consts.tile([P, 1], F32)
        nc.vector.memset(table_in[:], 0.0)
        nc.scalar.activation(out=table_out[:], in_=table_in[:], func=FUNC.Sigmoid)

        w_raw = resident.tile([P, PASSES, PACK, D], BF16)
        for q, pair in enumerate(((W_ii, W_if), (W_io, W_ig))):
            for slot, w_gate in enumerate(pair):
                nc.sync.dma_start(
                    out=w_raw[:, q, HALVES * slot : HALVES * (slot + 1), :],
                    in_=w_gate.rearrange("(c p) d -> p c d", p=P),
                )

        saved_sb = resident.tile([P, 2, N_TILES, H], BF16)
        gc_sb = resident.tile([P, N_TILES, H], BF16)
        gates_sb = []
        for first in range(0, N_TILES, SMALL_GROUP):
            group = slice(first, first + SMALL_GROUP)
            for r in range(first, first + SMALL_GROUP):
                gates_tile = gates_pool.tile([P, 4 * H], F32)
                nc.sync.dma_start(out=gates_tile[:], in_=gates_rows[:, r, :])
                gates_sb.append(gates_tile)
                if r == first:
                    nc.sync.dma_start(out=saved_sb[:, 0, group, :], in_=c0_rows[:, group, :])
                    nc.sync.dma_start(out=saved_sb[:, 1, group, :], in_=gh_rows[:, group, :])
                    nc.sync.dma_start(out=gc_sb[:, group, :], in_=gc_rows[:, group, :])

        w_grouped = resident.tile([P, PASSES, D, PACK], BF16, align_bytes=64)
        w_codes = resident.tile([P, PASSES, D], U32, align_bytes=64)
        w_scales = resident.tile([P, PASSES, D], U8, align_bytes=64)
        chunk = 0
        for q in range(PASSES):
            for d0 in range(0, D, W_CHUNK):
                dst = w_grouped[:, q, d0 : d0 + W_CHUNK, :].rearrange("p (b i) t -> p b t i", i=RUN)
                src = w_raw[:, q, :, d0 : d0 + W_CHUNK].rearrange("p t (b i) -> p b t i", i=RUN)
                if chunk % 3 == 2:
                    nc.scalar.copy(out=dst, in_=src)
                else:
                    nc.vector.tensor_copy(out=dst, in_=src)
                chunk += 1
        for q in range(PASSES):
            nc.vector.quantize_mx(
                out=w_codes[:, q, :].bitcast(E4M3_X4),
                scales=w_scales[:, q, :],
                in_=w_grouped[:, q].rearrange("p d t -> p (d t)"),
            )

        tiles = {}

        def activations(n):
            nat = ahead.tile([P, 5, H], F32)
            g = ahead.tile([P, H], F32)
            pre = gates_sb[n]
            nc.scalar.activation(out=nat[:, 1:4:2], in_=pre[:, col_i : col_i + 2 * H].rearrange("p (s h) -> p s h", s=2), func=FUNC.Sigmoid)
            nc.scalar.activation(out=g[:], in_=pre[:, col_g : col_g + H], func=FUNC.Tanh)
            nc.scalar.activation(out=nat[:, 4], in_=pre[:, col_o : col_o + H], func=FUNC.Sigmoid)
            nc.scalar.activation(out=nat[:, 2], in_=g[:], func=FUNC.Square)
            tiles["nat", n], tiles["g", n] = nat, g

        def products(n):
            prod_fo = natural.tile([P, 2, H], F32)
            nat = tiles["nat", n]
            nc.gpsimd.tensor_tensor(out=prod_fo[:], in0=nat[:, 3:5], in1=saved_sb[:, :, n, :], op=ALU.mult)
            nc.gpsimd.tensor_tensor(out=nat[:, 0], in0=nat[:, 1], in1=tiles["g", n][:], op=ALU.mult)
            tiles["prod_fo", n] = prod_fo

        def fo_factors(n):
            factor = natural.tile([P, 4, H], F32)
            nc.vector.scalar_tensor_tensor(
                out=factor[:, 1:3], in0=tiles["nat", n][:, 3:5], scalar=-1.0, in1=tiles["prod_fo", n][:],
                op0=ALU.add, op1=ALU.mult,
            )
            tiles["factor", n] = factor

        def ig_factors(n):
            nat = tiles["nat", n]
            nc.vector.scalar_tensor_tensor(
                out=tiles["factor", n][:, 0::3], in0=nat[:, 1:3], scalar=-1.0, in1=nat[:, 0:2],
                op0=ALU.add, op1=ALU.mult,
            )

        def transpose_cell(n):
            cell = psum_cell.tile([P, HALVES, P], F32)
            for c in range(HALVES):
                cols = slice(c * P, (c + 1) * P)
                nc.tensor.matmul(out=cell[:, c, :], lhsT=tiles["prod_fo", n][:, 0, cols], rhs=ident_f32[:], is_transpose=True, start=True, stop=False)
                nc.tensor.matmul(out=cell[:, c, :], lhsT=tiles["nat", n][:, 0, cols], rhs=ident_f32[:], is_transpose=True, start=False, stop=True)
            tiles["cell", n] = cell

        def transpose_grads(n):
            ogh = psum_ogh.tile([P, HALVES, P], F32)
            gc = psum_gc.tile([P, HALVES, P], BF16)
            for c in range(HALVES):
                cols = slice(c * P, (c + 1) * P)
                nc.tensor.transpose(ogh[:, c, :], tiles["prod_fo", n][:, 1, cols], ident_f32[:])
            for c in range(HALVES):
                cols = slice(c * P, (c + 1) * P)
                nc.tensor.transpose(gc[:, c, :], gc_sb[:, n, cols], ident_bf16[:])
            tiles["ogh", n], tiles["gc", n] = ogh, gc

        def transpose_factors(n, q):
            factor = tiles["factor", n]
            bank = psum_factor.tile([P, PACK, P], F32, tag="factor_t")
            for slot in range(2):
                for c in range(HALVES):
                    nc.tensor.transpose(
                        bank[:, HALVES * slot + c, :], factor[:, 2 * q + slot, c * P : (c + 1) * P], ident_f32[:]
                    )
            tiles["factor_t", n, q] = bank

        def cell_tanh(n):
            mult = ahead.tile([P, 2, HALVES, P], F32)
            nc.scalar.activation(out=mult[:, 0], in_=tiles["cell", n][:], func=FUNC.Tanh, scale=-1.0)
            tiles["mult", n] = mult

        def cell_square(n):
            th_sq = work.tile([P, HALVES, P], F32)
            nc.scalar.activation(out=th_sq[:], in_=tiles["mult", n][:, 0], func=FUNC.Square)
            tiles["th_sq", n] = th_sq

        def through_tanh(n):
            via_h = work.tile([P, HALVES, P], F32)
            nc.vector.scalar_tensor_tensor(
                out=via_h[:], in0=tiles["th_sq", n][:], scalar=-1.0, in1=tiles["ogh", n][:],
                op0=ALU.add, op1=ALU.mult,
            )
            tiles["via_h", n] = via_h

        def cell_gradient(n):
            nc.vector.tensor_tensor(out=tiles["mult", n][:, 1], in0=tiles["via_h", n][:], in1=tiles["gc", n][:], op=ALU.subtract)

        def gate_gradients(n, q):
            if q == 1:
                da_grouped = work.tile([P, PASSES, P, PACK], BF16, align_bytes=64)
                tiles["da_grouped", n] = da_grouped
            da_grouped, mult = tiles["da_grouped", n], tiles["mult", n]
            if q == 0:
                nc.vector.tensor_tensor(
                    out=da_grouped[:, q].rearrange("p n (s c) -> p n s c", s=2),
                    in0=tiles["factor_t", n, q][:].rearrange("p (s c) n -> p n s c", s=2),
                    in1=mult[:, 1].rearrange("p c n -> p n c").unsqueeze(2).to_broadcast([P, P, 2, HALVES]),
                    op=ALU.mult,
                )
            else:
                nc.vector.tensor_tensor(
                    out=da_grouped[:, q].rearrange("p (b i) t -> p b t i", i=RUN),
                    in0=tiles["factor_t", n, q][:].rearrange("p t (b i) -> p b t i", i=RUN),
                    in1=mult[:].rearrange("p s c n -> p (s c) n").rearrange("p t (b i) -> p b t i", i=RUN),
                    op=ALU.mult,
                )

        def quantise(n):
            da_codes = work.tile([P, PASSES * P], U32, align_bytes=64)
            da_scales = work.tile([P, PASSES * P], U8, align_bytes=64)
            nc.vector.quantize_mx(
                out=da_codes[:].bitcast(E5M2_X4),
                scales=da_scales[:],
                in_=tiles["da_grouped", n][:].rearrange("p q n t -> p (q n t)"),
            )
            tiles["da_codes", n], tiles["da_scales", n] = da_codes, da_scales

        def multiply(n):
            da_codes, da_scales = tiles["da_codes", n], tiles["da_scales", n]
            for bank in range(N_BANKS):
                acc = psum_out.tile([P, N_COLS], F32)
                cols = slice(bank * N_COLS, (bank + 1) * N_COLS)
                for q in range(PASSES):
                    toks = slice(q * P, (q + 1) * P)
                    nc.tensor.matmul_mx(
                        out=acc[:],
                        lhsT=da_codes[:, toks].bitcast(E5M2_X4),
                        lhsT_scale=da_scales[:, toks],
                        rhs=w_codes[:, q, cols].bitcast(E4M3_X4),
                        rhs_scale=w_scales[:, q, cols],
                        start=(q == 0),
                        stop=(q == PASSES - 1),
                    )
                tiles["acc", n, bank] = acc

        def empty_and_store(n, bank):
            out_sb = out_pool.tile([P, N_COLS], F32)
            if n == N_TILES - 1 and bank == N_BANKS - 1:
                nc.vector.tensor_copy(out=out_sb[:], in_=tiles["acc", n, bank][:])
            else:
                nc.scalar.copy(out=out_sb[:], in_=tiles["acc", n, bank][:])
            nc.sync.dma_start(out=out_rows[:, n, bank * N_COLS : (bank + 1) * N_COLS], in_=out_sb[:])

        def run(stage, n, *more):
            if 0 <= n < N_TILES:
                stage(n, *more)

        for r in range(-4, N_TILES + 1):
            run(activations, r + 4)
            run(products, r + 3)
            run(through_tanh, r + 1)
            run(gate_gradients, r, 1)
            run(gate_gradients, r, 0)
            run(cell_gradient, r + 1)
            run(transpose_cell, r + 2)
            run(cell_tanh, r + 2)
            run(transpose_factors, r + 1, 1)
            run(transpose_factors, r + 1, 0)
            run(transpose_grads, r + 2)
            run(quantise, r)
            run(fo_factors, r + 2)
            run(ig_factors, r + 2)
            run(empty_and_store, r - 1, 0)
            run(cell_square, r + 2)
            run(empty_and_store, r - 1, 1)
            run(multiply, r)
